import numpy as np
import ml_dtypes

BF16 = ml_dtypes.bfloat16


def bf(x):
    return np.asarray(x, np.float32).astype(BF16)


def f32(x):
    return np.asarray(x, np.float32)


def f64(x):
    return np.asarray(x).astype(np.float64)


def striped(idx):
    return np.tile(idx.reshape(-1, 16).T, (8, 1))


C, S, M, T, K, H, N = 128, 1024, 256, 3, 6, 512, 3072
EPS = 1e-5


def setup_inputs():
    sc = 1.0 / np.sqrt(T * C)
    return {"x": bf(np.random.standard_normal((C, S))), "w_self": bf(sc * np.random.standard_normal((C, M))), "w_left": bf(sc * np.random.standard_normal((C, M))), "w_right": bf(sc * np.random.standard_normal((C, M))), "b": f32(0.1 * np.random.standard_normal((M, 1))), "offs": striped(np.concatenate([np.random.permutation(S)[:H] for _ in range(K)]))}


def reference(x, w_self, w_left, w_right, b, offs):
    idx = offs[:16].T.reshape(-1)
    tap = idx.reshape(T, S)
    xs = f64(x)
    y = f64(w_self).T @ xs[:, tap[0]] + f64(w_left).T @ xs[:, tap[1]] + f64(w_right).T @ xs[:, tap[2]] + f64(b)
    mu = y.mean()
    sd = np.sqrt(np.square(y - mu).sum() / (M * S - 1))
    return np.maximum((y - mu) / (sd + EPS), 0.0)

@@ -1,0 +1,100 @@
+import concourse.mybir as mybir
+
+BF16, F32, U16 = mybir.dt.bfloat16, mybir.dt.float32, mybir.dt.uint16
+ALU = mybir.AluOpType
+ACT = mybir.ActivationFunctionType
+
+P = 128
+NODES = 1024
+FEATURES = 256
+TAPS = 3
+PIECE = 512
+BLOCKS = FEATURES // P
+HALVES = NODES // PIECE
+BANKS = BLOCKS * HALVES
+EPS = 1e-5
+
+FLOPS = 2 * TAPS * P * FEATURES * NODES
+
+
+def tile_net_latency_kernel(tc, x, w_self, w_left, w_right, b, offs, out):
+    nc = tc.nc
+    with (
+        tc.tile_pool(name="held", bufs=1) as held,
+        tc.tile_pool(name="result", bufs=BANKS) as result,
+        tc.psum_pool(name="psum", bufs=1) as psum,
+    ):
+        offsets = held.tile([P, TAPS * NODES // 16], U16, name="offsets")
+        nc.sync.dma_start(offsets[:], offs)
+        table = held.tile([P, NODES], BF16, name="table")
+        nc.scalar.dma_start(table[:], x)
+        weights = []
+        for tap, w in enumerate((w_self, w_left, w_right)):
+            w_tile = held.tile([P, FEATURES], BF16, name=f"w{tap}")
+            nc.sync.dma_start(w_tile[:], w)
+            weights.append(w_tile)
+        bias = held.tile([P, BLOCKS], F32, name="bias")
+        with nc.allow_non_contiguous_dma(reason="256 floats, one to a partition and block"):
+            nc.gpsimd.dma_start(bias[:], b.rearrange("(k p) o -> p (k o)", p=P))
+
+        averager = held.tile([P, P], F32, name="averager")
+        nc.vector.memset(averager[:], 1.0 / P)
+
+        stats = held.tile([P, BANKS * 6], F32, name="stats")
+        y = []
+        for block in range(BLOCKS):
+            for half in range(HALVES):
+                bank = block * HALVES + half
+                y_bank = psum.tile([P, PIECE], F32, name=f"y{bank}")
+                for tap in range(TAPS):
+                    first = (tap * NODES + half * PIECE) // 16
+                    nc.tensor.matmul(
+                        y_bank[:],
+                        weights[tap][:, block * P : (block + 1) * P],
+                        table[:].indirect(offsets[:, first : first + PIECE // 16]),
+                        start=(tap == 0),
+                        stop=(tap == TAPS - 1),
+                    )
+                nc.vector.bn_stats(stats[:, bank * 6 : (bank + 1) * 6], y_bank[:])
+                y.append(y_bank)
+            triples = stats[:, block * HALVES * 6 : (block + 1) * HALVES * 6]
+            means = triples.rearrange("p (t c) -> p t c", c=3)[:, :, 1:2]
+            nc.vector.tensor_scalar(means, means, bias[:, block : block + 1], None, ALU.add)
+
+        row = held.tile([P, 2], F32, name="row")
+        nc.vector.bn_aggr(row[:], stats[:])
+        row_mean, row_var = row[:, 0:1], row[:, 1:2]
+        mu_psum = psum.tile([P, 1], F32, name="mu_psum")
+        nc.tensor.matmul(mu_psum[:], averager[:], row_mean, start=True, stop=True)
+        var_psum = psum.tile([P, 1], F32, name="var_psum")
+        nc.tensor.matmul(var_psum[:], averager[:], row_var, start=True, stop=False)
+        mu = held.tile([P, 1], F32, name="mu")
+        nc.vector.tensor_copy(mu[:], mu_psum[:])
+        off_mean = held.tile([P, 1], F32, name="off_mean")
+        nc.vector.tensor_tensor(off_mean[:], row_mean, mu[:], ALU.subtract)
+        off_mean_sq = held.tile([P, 1], F32, name="off_mean_sq")
+        nc.vector.tensor_tensor(off_mean_sq[:], off_mean[:], off_mean[:], ALU.mult)
+        nc.tensor.matmul(var_psum[:], averager[:], off_mean_sq[:], start=False, stop=True)
+
+        n = FEATURES * NODES
+        sd = held.tile([P, 1], F32, name="sd")
+        nc.scalar.activation(sd[:], var_psum[:], ACT.Sqrt, scale=n / (n - 1.0))
+        gain = held.tile([P, 1], F32, name="gain")
+        nc.vector.tensor_scalar(gain[:], sd[:], EPS, None, ALU.add)
+        nc.vector.reciprocal(gain[:], gain[:])
+        shift = held.tile([P, BLOCKS], F32, name="shift")
+        nc.vector.tensor_scalar(shift[:], bias[:], mu[:], gain[:], ALU.subtract, ALU.mult)
+
+        for block in range(BLOCKS):
+            for half in range(HALVES):
+                normed = result.tile([P, PIECE], F32, name="normed")
+                nc.scalar.activation(
+                    normed[:],
+                    y[block * HALVES + half][:],
+                    ACT.Relu,
+                    bias=shift[:, block : block + 1],
+                    scale=gain[:],
+                )
+                nc.sync.dma_start(
+                    out[block * P : (block + 1) * P, half * PIECE : (half + 1) * PIECE], normed[:]
+                )

@@ -13,6 +13,7 @@ BLOCKS = FEATURES // P
 HALVES = NODES // PIECE
 BANKS = BLOCKS * HALVES
 EPS = 1e-5
+WARM_UPS = 5
 
 FLOPS = 2 * TAPS * P * FEATURES * NODES
 
@@ -39,6 +40,12 @@ def tile_net_latency_kernel(tc, x, w_self, w_left, w_right, b, offs, out):
 
         averager = held.tile([P, P], F32, name="averager")
         nc.vector.memset(averager[:], 1.0 / P)
+
+        zeros = held.tile([P, PIECE], BF16, name="zeros")
+        nc.gpsimd.memset(zeros[:], 0.0)
+        unread = psum.tile([P, PIECE], F32, name="unread")
+        for repeat in range(WARM_UPS):
+            nc.tensor.matmul(unread[:], zeros[:, 0:P], zeros[:], start=True, stop=True)
 
         stats = held.tile([P, BANKS * 6], F32, name="stats")
         y = []

@@ -13,7 +13,7 @@ BLOCKS = FEATURES // P
 HALVES = NODES // PIECE
 BANKS = BLOCKS * HALVES
 EPS = 1e-5
-WARM_UPS = 5
+WARM_UPS = 4
 
 FLOPS = 2 * TAPS * P * FEATURES * NODES
 
@@ -36,16 +36,16 @@ def tile_net_latency_kernel(tc, x, w_self, w_left, w_right, b, offs, out):
             weights.append(w_tile)
         bias = held.tile([P, BLOCKS], F32, name="bias")
         with nc.allow_non_contiguous_dma(reason="256 floats, one to a partition and block"):
-            nc.gpsimd.dma_start(bias[:], b.rearrange("(k p) o -> p (k o)", p=P))
-
-        averager = held.tile([P, P], F32, name="averager")
-        nc.vector.memset(averager[:], 1.0 / P)
+            nc.sync.dma_start(bias[:], b.rearrange("(k p) o -> p (k o)", p=P))
 
         zeros = held.tile([P, PIECE], BF16, name="zeros")
-        nc.gpsimd.memset(zeros[:], 0.0)
+        nc.vector.memset(zeros[:], 0.0)
         unread = psum.tile([P, PIECE], F32, name="unread")
         for repeat in range(WARM_UPS):
             nc.tensor.matmul(unread[:], zeros[:, 0:P], zeros[:], start=True, stop=True)
+
+        averager = held.tile([P, P], F32, name="averager")
+        nc.vector.memset(averager[:], 1.0 / P)
 
         stats = held.tile([P, BANKS * 6], F32, name="stats")
         y = []

@@ -8,12 +8,14 @@ P = 128
 NODES = 1024
 FEATURES = 256
 TAPS = 3
-PIECE = 512
 BLOCKS = FEATURES // P
-HALVES = NODES // PIECE
-BANKS = BLOCKS * HALVES
 EPS = 1e-5
-WARM_UPS = 4
+
+PIECES = (
+    ((0, 512), (512, 512)),
+    ((0, 512), (512, 384), (896, 128)),
+)
+N_PIECES = sum(len(cut) for cut in PIECES)
 
 FLOPS = 2 * TAPS * P * FEATURES * NODES
 
@@ -22,7 +24,6 @@ def tile_net_latency_kernel(tc, x, w_self, w_left, w_right, b, offs, out):
     nc = tc.nc
     with (
         tc.tile_pool(name="held", bufs=1) as held,
-        tc.tile_pool(name="result", bufs=BANKS) as result,
         tc.psum_pool(name="psum", bufs=1) as psum,
     ):
         offsets = held.tile([P, TAPS * NODES // 16], U16, name="offsets")
@@ -38,33 +39,27 @@ def tile_net_latency_kernel(tc, x, w_self, w_left, w_right, b, offs, out):
         with nc.allow_non_contiguous_dma(reason="256 floats, one to a partition and block"):
             nc.sync.dma_start(bias[:], b.rearrange("(k p) o -> p (k o)", p=P))
 
-        zeros = held.tile([P, PIECE], BF16, name="zeros")
-        nc.vector.memset(zeros[:], 0.0)
-        unread = psum.tile([P, PIECE], F32, name="unread")
-        for repeat in range(WARM_UPS):
-            nc.tensor.matmul(unread[:], zeros[:, 0:P], zeros[:], start=True, stop=True)
-
         averager = held.tile([P, P], F32, name="averager")
         nc.vector.memset(averager[:], 1.0 / P)
 
-        stats = held.tile([P, BANKS * 6], F32, name="stats")
+        stats = held.tile([P, N_PIECES * 6], F32, name="stats")
         y = []
-        for block in range(BLOCKS):
-            for half in range(HALVES):
-                bank = block * HALVES + half
-                y_bank = psum.tile([P, PIECE], F32, name=f"y{bank}")
+        for block, cut in enumerate(PIECES):
+            block_start = len(y) * 6
+            for first, nodes in cut:
+                y_piece = psum.tile([P, nodes], F32, name=f"y{len(y)}")
                 for tap in range(TAPS):
-                    first = (tap * NODES + half * PIECE) // 16
+                    column = (tap * NODES + first) // 16
                     nc.tensor.matmul(
-                        y_bank[:],
+                        y_piece[:],
                         weights[tap][:, block * P : (block + 1) * P],
-                        table[:].indirect(offsets[:, first : first + PIECE // 16]),
+                        table[:].indirect(offsets[:, column : column + nodes // 16]),
                         start=(tap == 0),
                         stop=(tap == TAPS - 1),
                     )
-                nc.vector.bn_stats(stats[:, bank * 6 : (bank + 1) * 6], y_bank[:])
-                y.append(y_bank)
-            triples = stats[:, block * HALVES * 6 : (block + 1) * HALVES * 6]
+                nc.vector.bn_stats(stats[:, len(y) * 6 : (len(y) + 1) * 6], y_piece[:])
+                y.append((block, first, nodes, y_piece))
+            triples = stats[:, block_start : len(y) * 6]
             means = triples.rearrange("p (t c) -> p t c", c=3)[:, :, 1:2]
             nc.vector.tensor_scalar(means, means, bias[:, block : block + 1], None, ALU.add)
 
@@ -75,13 +70,13 @@ def tile_net_latency_kernel(tc, x, w_self, w_left, w_right, b, offs, out):
         nc.tensor.matmul(mu_psum[:], averager[:], row_mean, start=True, stop=True)
         var_psum = psum.tile([P, 1], F32, name="var_psum")
         nc.tensor.matmul(var_psum[:], averager[:], row_var, start=True, stop=False)
-        mu = held.tile([P, 1], F32, name="mu")
-        nc.vector.tensor_copy(mu[:], mu_psum[:])
         off_mean = held.tile([P, 1], F32, name="off_mean")
-        nc.vector.tensor_tensor(off_mean[:], row_mean, mu[:], ALU.subtract)
+        nc.vector.tensor_tensor(off_mean[:], row_mean, mu_psum[:], ALU.subtract)
         off_mean_sq = held.tile([P, 1], F32, name="off_mean_sq")
         nc.vector.tensor_tensor(off_mean_sq[:], off_mean[:], off_mean[:], ALU.mult)
         nc.tensor.matmul(var_psum[:], averager[:], off_mean_sq[:], start=False, stop=True)
+        centre = held.tile([P, BLOCKS], F32, name="centre")
+        nc.vector.tensor_scalar(centre[:], bias[:], mu_psum[:], None, ALU.subtract)
 
         n = FEATURES * NODES
         sd = held.tile([P, 1], F32, name="sd")
@@ -90,18 +85,11 @@ def tile_net_latency_kernel(tc, x, w_self, w_left, w_right, b, offs, out):
         nc.vector.tensor_scalar(gain[:], sd[:], EPS, None, ALU.add)
         nc.vector.reciprocal(gain[:], gain[:])
         shift = held.tile([P, BLOCKS], F32, name="shift")
-        nc.vector.tensor_scalar(shift[:], bias[:], mu[:], gain[:], ALU.subtract, ALU.mult)
+        nc.vector.tensor_scalar(shift[:], centre[:], gain[:], None, ALU.mult)
 
-        for block in range(BLOCKS):
-            for half in range(HALVES):
-                normed = result.tile([P, PIECE], F32, name="normed")
-                nc.scalar.activation(
-                    normed[:],
-                    y[block * HALVES + half][:],
-                    ACT.Relu,
-                    bias=shift[:, block : block + 1],
-                    scale=gain[:],
-                )
-                nc.sync.dma_start(
-                    out[block * P : (block + 1) * P, half * PIECE : (half + 1) * PIECE], normed[:]
-                )
+        for block, first, nodes, y_piece in y:
+            normed = held.tile([P, nodes], F32, name=f"normed{block}_{first}")
+            nc.scalar.activation(
+                normed[:], y_piece[:], ACT.Relu, bias=shift[:, block : block + 1], scale=gain[:]
+            )
+            nc.sync.dma_start(out[block * P : (block + 1) * P, first : first + nodes], normed[:])

@@ -41,6 +41,17 @@ def tile_net_latency_kernel(tc, x, w_self, w_left, w_right, b, offs, out):
 
         averager = held.tile([P, P], F32, name="averager")
         nc.vector.memset(averager[:], 1.0 / P)
+        centring = held.tile([P, P], F32, name="centring")
+        nc.gpsimd.memset(centring[:], -1.0 / P)
+        nc.gpsimd.affine_select(
+            out=centring[:],
+            in_=centring[:],
+            compare_op=ALU.not_equal,
+            fill=1.0 - 1.0 / P,
+            base=0,
+            pattern=[[-1, P]],
+            channel_multiplier=1,
+        )
 
         stats = held.tile([P, N_PIECES * 6], F32, name="stats")
         y = []
@@ -66,17 +77,16 @@ def tile_net_latency_kernel(tc, x, w_self, w_left, w_right, b, offs, out):
         row = held.tile([P, 2], F32, name="row")
         nc.vector.bn_aggr(row[:], stats[:])
         row_mean, row_var = row[:, 0:1], row[:, 1:2]
-        mu_psum = psum.tile([P, 1], F32, name="mu_psum")
-        nc.tensor.matmul(mu_psum[:], averager[:], row_mean, start=True, stop=True)
+        off_mean = psum.tile([P, 1], F32, name="off_mean")
+        nc.tensor.matmul(off_mean[:], centring[:], row_mean, start=True, stop=True)
+        spread = held.tile([P, 1], F32, name="spread")
+        nc.vector.scalar_tensor_tensor(
+            spread[:], off_mean[:], off_mean[:], row_var, ALU.mult, ALU.add
+        )
         var_psum = psum.tile([P, 1], F32, name="var_psum")
-        nc.tensor.matmul(var_psum[:], averager[:], row_var, start=True, stop=False)
-        off_mean = held.tile([P, 1], F32, name="off_mean")
-        nc.vector.tensor_tensor(off_mean[:], row_mean, mu_psum[:], ALU.subtract)
-        off_mean_sq = held.tile([P, 1], F32, name="off_mean_sq")
-        nc.vector.tensor_tensor(off_mean_sq[:], off_mean[:], off_mean[:], ALU.mult)
-        nc.tensor.matmul(var_psum[:], averager[:], off_mean_sq[:], start=False, stop=True)
+        nc.tensor.matmul(var_psum[:], averager[:], spread[:], start=True, stop=True)
         centre = held.tile([P, BLOCKS], F32, name="centre")
-        nc.vector.tensor_scalar(centre[:], bias[:], mu_psum[:], None, ALU.subtract)
+        nc.vector.tensor_scalar(centre[:], bias[:], row_mean, off_mean[:], ALU.subtract, ALU.add)
 
         n = FEATURES * NODES
         sd = held.tile([P, 1], F32, name="sd")

@@ -39,6 +39,10 @@ def tile_net_latency_kernel(tc, x, w_self, w_left, w_right, b, offs, out):
         with nc.allow_non_contiguous_dma(reason="256 floats, one to a partition and block"):
             nc.sync.dma_start(bias[:], b.rearrange("(k p) o -> p (k o)", p=P))
 
+        last_bias = bias[:, BLOCKS - 1 : BLOCKS]
+        rel_bias = held.tile([P, BLOCKS], F32, name="rel_bias")
+        nc.vector.tensor_scalar(rel_bias[:], bias[:], last_bias, None, ALU.subtract)
+
         averager = held.tile([P, P], F32, name="averager")
         nc.vector.memset(averager[:], 1.0 / P)
         centring = held.tile([P, P], F32, name="centring")
@@ -70,15 +74,17 @@ def tile_net_latency_kernel(tc, x, w_self, w_left, w_right, b, offs, out):
                     )
                 nc.vector.bn_stats(stats[:, len(y) * 6 : (len(y) + 1) * 6], y_piece[:])
                 y.append((block, first, nodes, y_piece))
-            triples = stats[:, block_start : len(y) * 6]
-            means = triples.rearrange("p (t c) -> p t c", c=3)[:, :, 1:2]
-            nc.vector.tensor_scalar(means, means, bias[:, block : block + 1], None, ALU.add)
+            if block < BLOCKS - 1:
+                triples = stats[:, block_start : len(y) * 6]
+                means = triples.rearrange("p (t c) -> p t c", c=3)[:, :, 1:2]
+                nc.vector.tensor_scalar(means, means, rel_bias[:, block : block + 1], None, ALU.add)
 
         row = held.tile([P, 2], F32, name="row")
         nc.vector.bn_aggr(row[:], stats[:])
         row_mean, row_var = row[:, 0:1], row[:, 1:2]
         off_mean = psum.tile([P, 1], F32, name="off_mean")
-        nc.tensor.matmul(off_mean[:], centring[:], row_mean, start=True, stop=True)
+        nc.tensor.matmul(off_mean[:], centring[:], last_bias, start=True, stop=False)
+        nc.tensor.matmul(off_mean[:], centring[:], row_mean, start=False, stop=True)
         spread = held.tile([P, 1], F32, name="spread")
         nc.vector.scalar_tensor_tensor(
             spread[:], off_mean[:], off_mean[:], row_var, ALU.mult, ALU.add
@@ -86,7 +92,7 @@ def tile_net_latency_kernel(tc, x, w_self, w_left, w_right, b, offs, out):
         var_psum = psum.tile([P, 1], F32, name="var_psum")
         nc.tensor.matmul(var_psum[:], averager[:], spread[:], start=True, stop=True)
         centre = held.tile([P, BLOCKS], F32, name="centre")
-        nc.vector.tensor_scalar(centre[:], bias[:], row_mean, off_mean[:], ALU.subtract, ALU.add)
+        nc.vector.tensor_scalar(centre[:], rel_bias[:], row_mean, off_mean[:], ALU.subtract, ALU.add)
 
         n = FEATURES * NODES
         sd = held.tile([P, 1], F32, name="sd")

@@ -9,6 +9,7 @@ NODES = 1024
 FEATURES = 256
 TAPS = 3
 BLOCKS = FEATURES // P
+BANK = 512
 EPS = 1e-5
 
 PIECES = (
@@ -93,6 +94,13 @@ def tile_net_latency_kernel(tc, x, w_self, w_left, w_right, b, offs, out):
         nc.tensor.matmul(var_psum[:], averager[:], spread[:], start=True, stop=True)
         centre = held.tile([P, BLOCKS], F32, name="centre")
         nc.vector.tensor_scalar(centre[:], rel_bias[:], row_mean, off_mean[:], ALU.subtract, ALU.add)
+        short = [piece for piece in y if piece[2] < BANK]
+        whole = [piece for piece in y if piece[2] == BANK]
+        centred = []
+        for block, first, nodes, y_piece in short:
+            y_less_mu = held.tile([P, nodes], F32, name=f"normed{block}_{first}")
+            nc.vector.tensor_scalar(y_less_mu[:], y_piece[:], centre[:, block : block + 1], None, ALU.add)
+            centred.append(y_less_mu)
 
         n = FEATURES * NODES
         sd = held.tile([P, 1], F32, name="sd")
@@ -103,7 +111,10 @@ def tile_net_latency_kernel(tc, x, w_self, w_left, w_right, b, offs, out):
         shift = held.tile([P, BLOCKS], F32, name="shift")
         nc.vector.tensor_scalar(shift[:], centre[:], gain[:], None, ALU.mult)
 
-        for block, first, nodes, y_piece in y:
+        for (block, first, nodes, y_piece), y_less_mu in zip(short, centred):
+            nc.vector.tensor_scalar(y_less_mu[:], y_less_mu[:], gain[:], 0.0, ALU.mult, ALU.max)
+            nc.sync.dma_start(out[block * P : (block + 1) * P, first : first + nodes], y_less_mu[:])
+        for block, first, nodes, y_piece in whole:
             normed = held.tile([P, nodes], F32, name=f"normed{block}_{first}")
             nc.scalar.activation(
                 normed[:], y_piece[:], ACT.Relu, bias=shift[:, block : block + 1], scale=gain[:]

@@ -58,6 +58,11 @@ def tile_net_latency_kernel(tc, x, w_self, w_left, w_right, b, offs, out):
             channel_multiplier=1,
         )
 
+        n = FEATURES * NODES
+        bessel = n / (n - 1.0)
+        spread = held.tile([P, 2], F32, name="spread")
+        nc.vector.memset(spread[:, 1:2], EPS * EPS / bessel)
+
         stats = held.tile([P, N_PIECES * 6], F32, name="stats")
         y = []
         for block, cut in enumerate(PIECES):
@@ -86,11 +91,10 @@ def tile_net_latency_kernel(tc, x, w_self, w_left, w_right, b, offs, out):
         off_mean = psum.tile([P, 1], F32, name="off_mean")
         nc.tensor.matmul(off_mean[:], centring[:], last_bias, start=True, stop=False)
         nc.tensor.matmul(off_mean[:], centring[:], row_mean, start=False, stop=True)
-        spread = held.tile([P, 1], F32, name="spread")
         nc.vector.scalar_tensor_tensor(
-            spread[:], off_mean[:], off_mean[:], row_var, ALU.mult, ALU.add
+            spread[:, 0:1], off_mean[:], off_mean[:], row_var, ALU.mult, ALU.add
         )
-        var_psum = psum.tile([P, 1], F32, name="var_psum")
+        var_psum = psum.tile([P, 2], F32, name="var_psum")
         nc.tensor.matmul(var_psum[:], averager[:], spread[:], start=True, stop=True)
         centre = held.tile([P, BLOCKS], F32, name="centre")
         nc.vector.tensor_scalar(centre[:], rel_bias[:], row_mean, off_mean[:], ALU.subtract, ALU.add)
@@ -102,12 +106,11 @@ def tile_net_latency_kernel(tc, x, w_self, w_left, w_right, b, offs, out):
             nc.vector.tensor_scalar(y_less_mu[:], y_piece[:], centre[:, block : block + 1], None, ALU.add)
             centred.append(y_less_mu)
 
-        n = FEATURES * NODES
-        sd = held.tile([P, 1], F32, name="sd")
-        nc.scalar.activation(sd[:], var_psum[:], ACT.Sqrt, scale=n / (n - 1.0))
+        roots = held.tile([P, 2], F32, name="roots")
+        sd_eps = held.tile([P, 1], F32, name="sd_eps")
+        nc.scalar.activation(roots[:], var_psum[:], ACT.Sqrt, scale=bessel, accum_out=sd_eps[:])
         gain = held.tile([P, 1], F32, name="gain")
-        nc.vector.tensor_scalar(gain[:], sd[:], EPS, None, ALU.add)
-        nc.vector.reciprocal(gain[:], gain[:])
+        nc.vector.reciprocal(gain[:], sd_eps[:])
         shift = held.tile([P, BLOCKS], F32, name="shift")
         nc.vector.tensor_scalar(shift[:], centre[:], gain[:], None, ALU.mult)
 

@@ -67,19 +67,24 @@ def tile_net_latency_kernel(tc, x, w_self, w_left, w_right, b, offs, out):
         y = []
         for block, cut in enumerate(PIECES):
             block_start = len(y) * 6
-            for first, nodes in cut:
-                y_piece = psum.tile([P, nodes], F32, name=f"y{len(y)}")
-                for tap in range(TAPS):
-                    column = (tap * NODES + first) // 16
-                    nc.tensor.matmul(
-                        y_piece[:],
-                        weights[tap][:, block * P : (block + 1) * P],
-                        table[:].indirect(offsets[:, column : column + nodes // 16]),
-                        start=(tap == 0),
-                        stop=(tap == TAPS - 1),
-                    )
-                nc.vector.bn_stats(stats[:, len(y) * 6 : (len(y) + 1) * 6], y_piece[:])
-                y.append((block, first, nodes, y_piece))
+            banks = [psum.tile([P, nodes], F32, name=f"y{len(y) + i}") for i, (first, nodes) in enumerate(cut)]
+            if block < BLOCKS - 1:
+                order = [(tap, i) for tap in range(TAPS) for i in range(len(cut))]
+            else:
+                order = [(tap, i) for i in range(len(cut)) for tap in range(TAPS)]
+            for tap, i in order:
+                first, nodes = cut[i]
+                column = (tap * NODES + first) // 16
+                nc.tensor.matmul(
+                    banks[i][:],
+                    weights[tap][:, block * P : (block + 1) * P],
+                    table[:].indirect(offsets[:, column : column + nodes // 16]),
+                    start=(tap == 0),
+                    stop=(tap == TAPS - 1),
+                )
+                if tap == TAPS - 1:
+                    nc.vector.bn_stats(stats[:, len(y) * 6 : (len(y) + 1) * 6], banks[i][:])
+                    y.append((block, first, nodes, banks[i]))
             if block < BLOCKS - 1:
                 triples = stats[:, block_start : len(y) * 6]
                 means = triples.rearrange("p (t c) -> p t c", c=3)[:, :, 1:2]

import concourse.mybir as mybir

BF16, F32, U16 = mybir.dt.bfloat16, mybir.dt.float32, mybir.dt.uint16
ALU = mybir.AluOpType
ACT = mybir.ActivationFunctionType

P = 128
NODES = 1024
FEATURES = 256
TAPS = 3
BLOCKS = FEATURES // P
BANK = 512
EPS = 1e-5

PIECES = (
    ((0, 512), (512, 512)),
    ((0, 512), (512, 384), (896, 128)),
)
N_PIECES = sum(len(cut) for cut in PIECES)

FLOPS = 2 * TAPS * P * FEATURES * NODES


def tile_net_latency_kernel(tc, x, w_self, w_left, w_right, b, offs, out):
    nc = tc.nc
    with (
        tc.tile_pool(name="held", bufs=1) as held,
        tc.psum_pool(name="psum", bufs=1) as psum,
    ):
        offsets = held.tile([P, TAPS * NODES // 16], U16, name="offsets")
        nc.sync.dma_start(offsets[:], offs)
        table = held.tile([P, NODES], BF16, name="table")
        nc.scalar.dma_start(table[:], x)
        weights = []
        for tap, w in enumerate((w_self, w_left, w_right)):
            w_tile = held.tile([P, FEATURES], BF16, name=f"w{tap}")
            nc.sync.dma_start(w_tile[:], w)
            weights.append(w_tile)
        bias = held.tile([P, BLOCKS], F32, name="bias")
        with nc.allow_non_contiguous_dma(reason="256 floats, one to a partition and block"):
            nc.sync.dma_start(bias[:], b.rearrange("(k p) o -> p (k o)", p=P))

        last_bias = bias[:, BLOCKS - 1 : BLOCKS]
        rel_bias = held.tile([P, BLOCKS], F32, name="rel_bias")
        nc.vector.tensor_scalar(rel_bias[:], bias[:], last_bias, None, ALU.subtract)

        averager = held.tile([P, P], F32, name="averager")
        nc.vector.memset(averager[:], 1.0 / P)
        centring = held.tile([P, P], F32, name="centring")
        nc.gpsimd.memset(centring[:], -1.0 / P)
        nc.gpsimd.affine_select(
            out=centring[:],
            in_=centring[:],
            compare_op=ALU.not_equal,
            fill=1.0 - 1.0 / P,
            base=0,
            pattern=[[-1, P]],
            channel_multiplier=1,
        )

        n = FEATURES * NODES
        bessel = n / (n - 1.0)
        spread = held.tile([P, 2], F32, name="spread")
        nc.vector.memset(spread[:, 1:2], EPS * EPS / bessel)

        stats = held.tile([P, N_PIECES * 6], F32, name="stats")
        y = []
        for block, cut in enumerate(PIECES):
            block_start = len(y) * 6
            banks = [psum.tile([P, nodes], F32, name=f"y{len(y) + i}") for i, (first, nodes) in enumerate(cut)]
            if block < BLOCKS - 1:
                order = [(tap, i) for tap in range(TAPS) for i in range(len(cut))]
            else:
                order = [(tap, i) for i in range(len(cut)) for tap in range(TAPS)]
            for tap, i in order:
                first, nodes = cut[i]
                column = (tap * NODES + first) // 16
                nc.tensor.matmul(
                    banks[i][:],
                    weights[tap][:, block * P : (block + 1) * P],
                    table[:].indirect(offsets[:, column : column + nodes // 16]),
                    start=(tap == 0),
                    stop=(tap == TAPS - 1),
                )
                if tap == TAPS - 1:
                    nc.vector.bn_stats(stats[:, len(y) * 6 : (len(y) + 1) * 6], banks[i][:])
                    y.append((block, first, nodes, banks[i]))
            if block < BLOCKS - 1:
                triples = stats[:, block_start : len(y) * 6]
                means = triples.rearrange("p (t c) -> p t c", c=3)[:, :, 1:2]
                nc.vector.tensor_scalar(means, means, rel_bias[:, block : block + 1], None, ALU.add)

        row = held.tile([P, 2], F32, name="row")
        nc.vector.bn_aggr(row[:], stats[:])
        row_mean, row_var = row[:, 0:1], row[:, 1:2]
        off_mean = psum.tile([P, 1], F32, name="off_mean")
        nc.tensor.matmul(off_mean[:], centring[:], last_bias, start=True, stop=False)
        nc.tensor.matmul(off_mean[:], centring[:], row_mean, start=False, stop=True)
        nc.vector.scalar_tensor_tensor(
            spread[:, 0:1], off_mean[:], off_mean[:], row_var, ALU.mult, ALU.add
        )
        var_psum = psum.tile([P, 2], F32, name="var_psum")
        nc.tensor.matmul(var_psum[:], averager[:], spread[:], start=True, stop=True)
        centre = held.tile([P, BLOCKS], F32, name="centre")
        nc.vector.tensor_scalar(centre[:], rel_bias[:], row_mean, off_mean[:], ALU.subtract, ALU.add)
        short = [piece for piece in y if piece[2] < BANK]
        whole = [piece for piece in y if piece[2] == BANK]
        centred = []
        for block, first, nodes, y_piece in short:
            y_less_mu = held.tile([P, nodes], F32, name=f"normed{block}_{first}")
            nc.vector.tensor_scalar(y_less_mu[:], y_piece[:], centre[:, block : block + 1], None, ALU.add)
            centred.append(y_less_mu)

        roots = held.tile([P, 2], F32, name="roots")
        sd_eps = held.tile([P, 1], F32, name="sd_eps")
        nc.scalar.activation(roots[:], var_psum[:], ACT.Sqrt, scale=bessel, accum_out=sd_eps[:])
        gain = held.tile([P, 1], F32, name="gain")
        nc.vector.reciprocal(gain[:], sd_eps[:])
        shift = held.tile([P, BLOCKS], F32, name="shift")
        nc.vector.tensor_scalar(shift[:], centre[:], gain[:], None, ALU.mult)

        for (block, first, nodes, y_piece), y_less_mu in zip(short, centred):
            nc.vector.tensor_scalar(y_less_mu[:], y_less_mu[:], gain[:], 0.0, ALU.mult, ALU.max)
            nc.sync.dma_start(out[block * P : (block + 1) * P, first : first + nodes], y_less_mu[:])
        for block, first, nodes, y_piece in whole:
            normed = held.tile([P, nodes], F32, name=f"normed{block}_{first}")
            nc.scalar.activation(
                normed[:], y_piece[:], ACT.Relu, bias=shift[:, block : block + 1], scale=gain[:]
            )
            nc.sync.dma_start(out[block * P : (block + 1) * P, first : first + nodes], normed[:])
